import numpy as np
import ml_dtypes


def mxq(x, axis, fmt="e4m3"):
    dtype, down = {"e4m3": (ml_dtypes.float8_e4m3fn, 7), "e5m2": (ml_dtypes.float8_e5m2, 14)}[fmt]
    v = np.moveaxis(np.asarray(x, np.float32).astype(ml_dtypes.bfloat16).astype(np.float64), axis, -1)
    blocks = v.reshape(v.shape[:-1] + (-1, 32))
    amax = np.abs(blocks).max(-1, keepdims=True)
    byte = np.maximum(np.where(amax > 0, np.frexp(amax)[1] - 1 + 127, 0) - down, 1)
    scale = np.exp2(byte - 127.0)
    codes = (blocks / scale).astype(np.float32).astype(dtype).astype(np.float64)
    return np.moveaxis((codes * scale).reshape(v.shape), -1, axis)


WIDE = False


def mx_kscale(k):
    if not WIDE:
        return np.ones(k)
    levels = np.array([10, -10, 5, -5, 0])
    if k % 512:
        return np.exp2(np.random.permutation(np.resize(levels, k // 32))).repeat(32)
    a = np.empty((k // 512, 16))
    for p in range(k // 512):
        a[p, :8] = np.random.permutation(np.resize(levels, 8))
        for g in range(8):
            far = levels[np.abs(levels - a[p, g]) >= 10]
            a[p, g + 8] = far[np.random.randint(len(far))]
    return np.exp2(a.ravel()).repeat(32)


BF16 = ml_dtypes.bfloat16


def bf(x):
    return np.asarray(x, np.float32).astype(BF16)


def f64(x):
    return np.asarray(x).astype(np.float64)


B, K, F, INCH, OUTCH, R = 2, 8, 256, 1024, 1024, 128


def erf(a):
    c = np.clip(a, -6.0, 6.0)
    c2 = 2.0 * c * c
    t = c.copy()
    s = c.copy()
    n = 1.0
    while np.max(np.abs(t) - 1e-18 * np.abs(s)) > 0.0:
        n += 2.0
        t = t * c2 / n
        s = s + t
    return 2.0 / np.sqrt(np.pi) * np.exp(-c * c) * s


def gelu(t):
    return 0.5 * t * (1.0 + erf(t / np.sqrt(2.0)))


def setup_inputs():
    s = mx_kscale(INCH)
    return {
        "h": bf(gelu(np.random.standard_normal((B, K, F, INCH))) * s),
        "z": bf(np.random.standard_normal((B, K, F, R)) * 0.35),
        "u": bf(np.random.standard_normal((B, K, OUTCH, R)) * 1.5 * np.sqrt(R)),
        "b": bf(np.random.standard_normal((B, 1, 1, OUTCH)) * 0.3),
        "W_out": bf(np.random.standard_normal((OUTCH, INCH)) * 1.5 / np.sqrt(INCH) / s),
        "b_out": bf(np.random.standard_normal(OUTCH) * 0.3),
    }


def reference(h, z, u, b, W_out, b_out):
    lora = f64(z) @ f64(u).transpose(0, 1, 3, 2) / R
    main = mxq(f64(h), 3, "e4m3") @ mxq(f64(W_out).T, 0, "e4m3")
    return gelu(main + f64(b_out) + lora + f64(b))

@@ -1,0 +1,324 @@
+from contextlib import ExitStack
+
+import concourse.mybir as mybir
+from concourse.masks import make_identity
+
+F32 = mybir.dt.float32
+BF16 = mybir.dt.bfloat16
+U32 = mybir.dt.uint32
+U8 = mybir.dt.uint8
+FP8X4 = mybir.dt.float8_e4m3fn_x4
+ACTF = mybir.ActivationFunctionType
+ALU = mybir.AluOpType
+
+FLOPS = 2 * 4096 * 1024 * 1024 + 2 * 4096 * 1024 * 128
+
+P = 128
+UNITS = 16
+DU = 6
+DL = 4
+DH = 2
+PRE_BUFS = 6
+W_STEP = -2.5
+W_AT = {-3: (0, 1), -2: (2, 3)}
+LOAD_AHEAD = 3
+MANUAL = True
+ACT_J = [(1, 2), (1,), (1,), (1,)]
+XU_ENG = "act"
+HEAD_ACT = (1, 3)
+XW_ACT = (0,)
+GROUP_LO = True
+
+
+def p1_engine(i, j):
+    if i < DL:
+        return "act" if j in HEAD_ACT else "dve"
+    return "act" if j in ACT_J[i % len(ACT_J)] else "dve"
+
+
+def tile_loratacmlp4_pb_t_kernel(tc, h, z, u, b, W_out, b_out, out):
+    nc = tc.nc
+    h_v = h.rearrange("a k (p t) c -> (a k) p (t c)", t=2)
+    z_v = z.rearrange("a k (p t) r -> p (a k) (t r)", t=2)
+    u_v = u.rearrange("a k (c p j) r -> (a k) p c (j r)", c=4, j=2)
+    w_v = W_out.rearrange("(c p j) k -> c p (j k)", c=4, j=2)
+    o_v = out.rearrange("a k (p t) o -> (a k) p t o", t=2)
+    b_v = b.rearrange("a x y o -> (x y) a o")
+    bo_v = b_out.rearrange("(x o) -> x o", x=1)
+
+    with ExitStack() as ctx:
+        const = ctx.enter_context(tc.tile_pool(name="const", bufs=1))
+        hpool = ctx.enter_context(tc.tile_pool(name="hpool", bufs=8))
+        upool = ctx.enter_context(tc.tile_pool(name="upool", bufs=8))
+        work = ctx.enter_context(tc.tile_pool(name="work", bufs=3))
+        prep = ctx.enter_context(tc.tile_pool(name="prep", bufs=PRE_BUFS))
+        stg = ctx.enter_context(tc.tile_pool(name="stg", bufs=6))
+        psum = ctx.enter_context(tc.psum_pool(name="psum", bufs=8))
+        if MANUAL:
+            ctx.enter_context(tc.manual_schedule())
+
+        def bank(shape, dtype, name):
+            return psum.tile(shape, dtype, name=name, tag="ps")
+
+        ident_f = const.tile([P, P], F32, name="ident_f")
+        ident_b = const.tile([P, P], BF16, name="ident_b")
+        make_identity(nc, ident_b[:])
+        make_identity(nc, ident_f[:])
+        ones = const.tile([P, P], BF16, name="ones")
+        nc.vector.memset(ones[:], 1.0)
+        bias_in = const.tile([P, 2, 1024], BF16, name="bias_in")
+        nc.vector.memset(bias_in[:], 0.0)
+        c128 = const.tile([P, P], BF16, name="c128")
+        nc.vector.memset(c128[:], 128.0)
+        bias_pm = const.tile([P, 2048], BF16, name="bias_pm")
+        warm = const.tile([P, 1], F32, name="warm")
+        nc.vector.memset(warm[:], 0.0)
+        nc.scalar.activation(out=warm[:], in_=warm[:], func=ACTF.Gelu)
+        nc.scalar.dma_start(out=bias_in[1:2, :, :], in_=b_v)
+        for a in range(2):
+            nc.scalar.dma_start(out=bias_in[0:1, a, :], in_=bo_v)
+
+        nc.vector.tensor_copy(out=bias_pm[:].rearrange("q (m j p) -> q m j p", m=8, j=2),
+                              in_=bias_in[:].rearrange("q a (c p j) -> q (a c) j p", c=4, j=2))
+
+        z_sb = [const.tile([P, 4, 256], BF16, name="z_sb%d" % k) for k in range(4)]
+        zT = [const.tile([P, 1024], BF16, name="zT%d" % k) for k in range(4)]
+        w_sb = [const.tile([P, 2048], BF16, name="w_sb%d" % c) for c in range(4)]
+        gW = [const.tile([P, 4096], BF16, name="gW%d" % n, align_bytes=64) for n in range(2)]
+        cW = [const.tile([P, 1024], U32, name="cW%d" % n, align_bytes=64) for n in range(2)]
+        sW = [const.tile([P, 1024], U8, name="sW%d" % n, align_bytes=64) for n in range(2)]
+        bias_sb = [const.tile([P, 1024], F32, name="bias_sb%d" % a) for a in range(2)]
+
+        h_sb, u_sb, hq, ch, sh, uT, pre, lo_ps, mx_ps, h_ps, u_ps = {}, {}, {}, {}, {}, {}, {}, {}, {}, {}, {}
+
+        def load_z(k):
+            nc.sync.dma_start(out=z_sb[k][:], in_=z_v[:, 4 * k : 4 * k + 4, :])
+
+        def load_w(c):
+            nc.sync.dma_start(out=w_sb[c][:], in_=w_v[c])
+
+        def load_u(i):
+            u_sb[i] = upool.tile([P, 4, 256], BF16, name="u_sb_%d" % i, tag="u")
+            nc.sync.dma_start(out=u_sb[i][:], in_=u_v[i])
+
+        def load_h(i):
+            h_sb[i] = hpool.tile([P, 2048], BF16, name="h_sb_%d" % i, tag="h")
+            nc.sync.dma_start(out=h_sb[i][:], in_=h_v[i])
+
+        def copy_on(eng, out_, in_):
+            if eng == "act":
+                nc.scalar.copy(out=out_, in_=in_)
+            else:
+                nc.vector.tensor_copy(out=out_, in_=in_)
+
+        def t_z(k):
+            ps = bank([P, 1024], BF16, "z_ps%d" % k)
+            for q in range(8):
+                nc.tensor.transpose(ps[:, q * P : (q + 1) * P], z_sb[k][:, q // 2, (q % 2) * P : (q % 2 + 1) * P], ident_b[:])
+            return ps
+
+        def x_z(k, ps, eng):
+            copy_on(eng, zT[k][:], ps[:])
+
+        def t_u(i, half):
+            if half == 0:
+                u_ps[i] = bank([P, 1024], BF16, "u_ps%d" % i)
+            ps = u_ps[i]
+            for q in range(4 * half, 4 * half + 4):
+                nc.tensor.transpose(ps[:, q * P : (q + 1) * P], u_sb[i][:, q // 2, (q % 2) * P : (q % 2 + 1) * P], ident_b[:])
+
+        def x_u(i, eng):
+            uT[i] = work.tile([P, 1024], BF16, name="uT_%d" % i, tag="uT", bufs=4)
+            copy_on(eng, uT[i][:], u_ps[i][:])
+
+        def words_T(src_f32, base, name):
+            ps = bank([P, 512], F32, name)
+            for q in range(4):
+                at = base + (q // 2) * 256 + q % 2
+                nc.tensor.transpose(ps[:, q * P : (q + 1) * P], src_f32[:, at : at + 255 : 2], ident_f[:])
+            return ps
+
+        def t_h(i, t):
+            h_ps[i, t] = words_T(h_sb[i][:].bitcast(F32), t * 512, "h_ps%d_%d" % (i, t))
+
+        def x_h(i, t, eng):
+            if t == 0:
+                hq[i] = work.tile([P, 2048], BF16, name="hq_%d" % i, tag="hq", align_bytes=64)
+            dst = hq[i][:].bitcast(F32)[:, t * 512 : (t + 1) * 512].rearrange("q (g f e) -> q g f e", g=2, e=2)
+            copy_on(eng, dst, h_ps[i, t][:].rearrange("q (g e f) -> q g f e", g=2, e=2))
+
+        def q_h(i):
+            ch[i] = work.tile([P, 512], U32, name="ch_%d" % i, tag="ch", align_bytes=64)
+            sh[i] = work.tile([P, 512], U8, name="sh_%d" % i, tag="sh", align_bytes=64)
+            nc.vector.quantize_mx(out=ch[i][:].bitcast(FP8X4), scales=sh[i][:], in_=hq[i][:])
+
+        def t_w(c, j):
+            return words_T(w_sb[c][:].bitcast(F32), j * 512, "w_ps%d_%d" % (c, j))
+
+        def x_w(c, j, ps, eng):
+            off = (c % 2) * 256 + j * P
+            dst = gW[c // 2][:].bitcast(F32).rearrange("q (g o e) -> q g o e", g=2, e=2)[:, :, off : off + P, :]
+            copy_on(eng, dst, ps[:].rearrange("q (g e o) -> q g o e", g=2, e=2))
+
+        def q_w(n):
+            nc.vector.quantize_mx(out=cW[n][:].bitcast(FP8X4), scales=sW[n][:], in_=gW[n][:])
+
+        def bias_mm(a, n):
+            ps = bank([P, 512], F32, "b_ps%d_%d" % (a, n))
+            nc.tensor.matmul(out=ps[:], lhsT=ones[:], rhs=bias_in[:, a, n * 512 : (n + 1) * 512], start=True, stop=True)
+            return ps
+
+        def bias_x(a, n, ps, eng):
+            dst = bias_sb[a][:, n * 512 : (n + 1) * 512].rearrange("q (c j p) -> q c j p", c=2, j=2)
+            copy_on(eng, dst, ps[:].rearrange("q (c p j) -> q c j p", c=2, j=2))
+
+        def lo(i, t, n):
+            ps = bank([P, 512], F32, "lo_ps%d_%d_%d" % (i, t, n))
+            q = (i % 4) * 2 + t
+            nc.tensor.matmul(out=ps[:], lhsT=zT[i // 4][:, q * P : (q + 1) * P], rhs=uT[i][:, n * 512 : (n + 1) * 512],
+                             start=True, stop=p1_engine(i, 2 * t + n) != "act")
+            lo_ps[i, t, n] = ps
+
+        def lo_bias(i, t, n):
+            m = (i // 8) * 2 + n
+            nc.tensor.matmul(out=lo_ps[i, t, n][:], lhsT=c128[:], rhs=bias_pm[:, m * 512 : (m + 1) * 512],
+                             start=False, stop=True)
+
+        def p1(i, t, n, eng):
+            if (i not in pre):
+                pre[i] = prep.tile([P, 2048], F32, name="pre_%d" % i, tag="pre")
+            dst = pre[i][:, t * 1024 + n * 512 : t * 1024 + (n + 1) * 512]
+            bia = bias_sb[i // 8][:, n * 512 : (n + 1) * 512]
+            if eng == "act":
+                nc.scalar.activation(out=dst, in_=lo_ps[i, t, n][:], func=ACTF.Copy, scale=1.0 / 128.0)
+            else:
+                nc.vector.scalar_tensor_tensor(out=dst, in0=lo_ps[i, t, n][:], scalar=1.0 / 128.0, in1=bia,
+                                               op0=ALU.mult, op1=ALU.add)
+
+        def mx(i, t, n):
+            ps = bank([P, 512], F32, "mx_ps%d_%d_%d" % (i, t, n))
+            for g in range(2):
+                q = 2 * t + g
+                nc.tensor.matmul_mx(out=ps[:], lhsT=ch[i][:, q * P : (q + 1) * P].bitcast(FP8X4),
+                                    lhsT_scale=sh[i][:, q * P : (q + 1) * P],
+                                    rhs=cW[n][:, g * 512 : (g + 1) * 512].bitcast(FP8X4),
+                                    rhs_scale=sW[n][:, g * 512 : (g + 1) * 512], start=(g == 0), stop=(g == 1))
+            mx_ps[i, t, n] = ps
+
+        def p2(i, t, n):
+            dst = pre[i][:, t * 1024 + n * 512 : t * 1024 + (n + 1) * 512]
+            nc.vector.tensor_tensor(out=dst, in0=mx_ps[i, t, n][:], in1=dst, op=ALU.add)
+
+        def ge(i, t):
+            st = stg.tile([P, 1024], F32, name="st_%d_%d" % (i, t), tag="st")
+            nc.scalar.activation(out=st[:].rearrange("q (c p j) -> q c p j", c=4, j=2),
+                                 in_=pre[i][:, t * 1024 : (t + 1) * 1024].rearrange("q (c j p) -> q c p j", c=4, j=2),
+                                 func=ACTF.Gelu)
+            nc.sync.dma_start(out=o_v[i][:, t, :], in_=st[:])
+
+        def ge_half(i, t, n):
+            st = stg.tile([P, 512], F32, name="sth_%d_%d_%d" % (i, t, n), tag="st")
+            lo_c = t * 1024 + n * 512
+            nc.scalar.activation(out=st[:].rearrange("q (c p j) -> q c p j", c=2, j=2),
+                                 in_=pre[i][:, lo_c : lo_c + 512].rearrange("q (c j p) -> q c p j", c=2, j=2),
+                                 func=ACTF.Gelu)
+            nc.sync.dma_start(out=o_v[i][:, t, n * 512 : (n + 1) * 512], in_=st[:])
+
+        loads = []
+        for i in range(UNITS):
+            loads.append((i - DU, 1, load_u, i))
+            loads.append((i - DH, 2, load_h, i))
+        for kk in range(4):
+            loads.append((4 * kk - DU, 0, load_z, kk))
+        for c in range(4):
+            loads.append((W_STEP - 0.5, c, load_w, c))
+        loads = sorted(loads, key=lambda e: (e[0], e[1]))
+        issued = [0]
+
+        def issue_loads(upto):
+            while issued[0] < len(loads) and loads[issued[0]][0] <= upto:
+                e = loads[issued[0]]
+                e[2](e[3])
+                issued[0] += 1
+
+        issue_loads(-DU + LOAD_AHEAD)
+        late_ge = None
+        for s in range(-DU, UNITS):
+            iu, il, ih = s + DU, s + DL, s + DH
+            runs = []
+            for c in W_AT.get(s, ()):
+                for j in range(2):
+                    runs.append(("w", c, j))
+            if 0 <= ih < UNITS:
+                runs.append(("h", ih, 0))
+                runs.append(("h", ih, 1))
+            if iu % 4 == 0 and iu < UNITS:
+                runs.append(("z", iu // 4, 0))
+            if iu < UNITS:
+                runs.append(("u", iu, 0))
+                runs.append(("u", iu, 1))
+            if il in (0, 8):
+                pb = [bias_mm(il // 8, n) for n in range(2)]
+                for n in range(2):
+                    bias_x(il // 8, n, pb[n], "dve")
+            slots = []
+            if 0 <= il < UNITS:
+                for j in range(4):
+                    slots.append(("lo", j))
+                    if p1_engine(il, j) == "act":
+                        slots.append(("bias", j))
+            gaps = max(len(slots) - 1, 1)
+            per_gap = (len(runs) + gaps - 1) // gaps
+            done = 0
+            for k in range(max(len(slots), 1)):
+                if slots:
+                    kind, j = slots[k]
+                    if kind == "lo":
+                        lo(il, j // 2, j % 2)
+                    else:
+                        lo_bias(il, j // 2, j % 2)
+                    if kind == "bias" or p1_engine(il, j) != "act":
+                        p1(il, j // 2, j % 2, p1_engine(il, j))
+                if k < gaps:
+                    todo = runs[done : done + per_gap]
+                    done += len(todo)
+                    held = []
+                    for kind, a, bb in todo:
+                        if kind == "w":
+                            held.append(t_w(a, bb))
+                        elif kind == "h":
+                            t_h(a, bb)
+                            held.append(None)
+                        elif kind == "z":
+                            held.append(t_z(a))
+                        else:
+                            t_u(a, bb)
+                            held.append(None)
+                    for (kind, a, bb), ps in zip(todo, held):
+                        if kind == "w":
+                            x_w(a, bb, ps, "act" if bb in XW_ACT else "dve")
+                            if bb == 1 and a % 2 == 1:
+                                q_w(a // 2)
+                        elif kind == "h":
+                            x_h(a, bb, "act")
+                        elif kind == "z":
+                            x_z(a, ps, XU_ENG)
+                        elif bb == 1:
+                            x_u(a, XU_ENG)
+            if late_ge is not None:
+                ge(*late_ge)
+                late_ge = None
+            issue_loads(s + 1 + LOAD_AHEAD)
+            for j in range(4):
+                t, n = j // 2, j % 2
+                if s >= 0:
+                    mx(s, t, n)
+                    p2(s, t, n)
+                    if s == UNITS - 1:
+                        ge_half(s, t, n)
+                    elif j == 1:
+                        ge(s, 0)
+            if 0 <= ih < UNITS:
+                q_h(ih)
+            if 0 <= s < UNITS - 1:
+                late_ge = (s, 1)

@@ -27,7 +27,7 @@ ACT_J = [(1, 2), (1,), (1,), (1,)]
 XU_ENG = "act"
 HEAD_ACT = (1, 3)
 XW_ACT = (0,)
-GROUP_LO = True
+LW = 256
 
 
 def p1_engine(i, j):
@@ -89,7 +89,7 @@ def tile_loratacmlp4_pb_t_kernel(tc, h, z, u, b, W_out, b_out, out):
         sW = [const.tile([P, 1024], U8, name="sW%d" % n, align_bytes=64) for n in range(2)]
         bias_sb = [const.tile([P, 1024], F32, name="bias_sb%d" % a) for a in range(2)]
 
-        h_sb, u_sb, hq, ch, sh, uT, pre, lo_ps, mx_ps, h_ps, u_ps = {}, {}, {}, {}, {}, {}, {}, {}, {}, {}, {}
+        h_sb, u_sb, hq, ch, sh, uT, pre, lo_ps, mx_ps, h_ps, u_ps, z_ps, w_ps = ({} for _ in range(13))
 
         def load_z(k):
             nc.sync.dma_start(out=z_sb[k][:], in_=z_v[:, 4 * k : 4 * k + 4, :])
@@ -111,35 +111,31 @@ def tile_loratacmlp4_pb_t_kernel(tc, h, z, u, b, W_out, b_out, out):
             else:
                 nc.vector.tensor_copy(out=out_, in_=in_)
 
-        def t_z(k):
-            ps = bank([P, 1024], BF16, "z_ps%d" % k)
-            for q in range(8):
-                nc.tensor.transpose(ps[:, q * P : (q + 1) * P], z_sb[k][:, q // 2, (q % 2) * P : (q % 2 + 1) * P], ident_b[:])
-            return ps
+        def t_z(k, q):
+            if q == 0:
+                z_ps[k] = bank([P, 1024], BF16, "z_ps%d" % k)
+            nc.tensor.transpose(z_ps[k][:, q * P : (q + 1) * P], z_sb[k][:, q // 2, (q % 2) * P : (q % 2 + 1) * P], ident_b[:])
 
-        def x_z(k, ps, eng):
-            copy_on(eng, zT[k][:], ps[:])
+        def x_z(k, eng):
+            copy_on(eng, zT[k][:], z_ps[k][:])
 
-        def t_u(i, half):
-            if half == 0:
+        def t_u(i, q):
+            if q == 0:
                 u_ps[i] = bank([P, 1024], BF16, "u_ps%d" % i)
-            ps = u_ps[i]
-            for q in range(4 * half, 4 * half + 4):
-                nc.tensor.transpose(ps[:, q * P : (q + 1) * P], u_sb[i][:, q // 2, (q % 2) * P : (q % 2 + 1) * P], ident_b[:])
+            nc.tensor.transpose(u_ps[i][:, q * P : (q + 1) * P], u_sb[i][:, q // 2, (q % 2) * P : (q % 2 + 1) * P], ident_b[:])
 
         def x_u(i, eng):
             uT[i] = work.tile([P, 1024], BF16, name="uT_%d" % i, tag="uT", bufs=4)
             copy_on(eng, uT[i][:], u_ps[i][:])
 
-        def words_T(src_f32, base, name):
-            ps = bank([P, 512], F32, name)
-            for q in range(4):
-                at = base + (q // 2) * 256 + q % 2
-                nc.tensor.transpose(ps[:, q * P : (q + 1) * P], src_f32[:, at : at + 255 : 2], ident_f[:])
-            return ps
+        def word_T(ps, src_f32, base, q):
+            at = base + (q // 2) * 256 + q % 2
+            nc.tensor.transpose(ps[:, q * P : (q + 1) * P], src_f32[:, at : at + 255 : 2], ident_f[:])
 
-        def t_h(i, t):
-            h_ps[i, t] = words_T(h_sb[i][:].bitcast(F32), t * 512, "h_ps%d_%d" % (i, t))
+        def t_h(i, t, q):
+            if q == 0:
+                h_ps[i, t] = bank([P, 512], F32, "h_ps%d_%d" % (i, t))
+            word_T(h_ps[i, t], h_sb[i][:].bitcast(F32), t * 512, q)
 
         def x_h(i, t, eng):
             if t == 0:
@@ -152,10 +148,13 @@ def tile_loratacmlp4_pb_t_kernel(tc, h, z, u, b, W_out, b_out, out):
             sh[i] = work.tile([P, 512], U8, name="sh_%d" % i, tag="sh", align_bytes=64)
             nc.vector.quantize_mx(out=ch[i][:].bitcast(FP8X4), scales=sh[i][:], in_=hq[i][:])
 
-        def t_w(c, j):
-            return words_T(w_sb[c][:].bitcast(F32), j * 512, "w_ps%d_%d" % (c, j))
+        def t_w(c, j, q):
+            if q == 0:
+                w_ps[c, j] = bank([P, 512], F32, "w_ps%d_%d" % (c, j))
+            word_T(w_ps[c, j], w_sb[c][:].bitcast(F32), j * 512, q)
 
-        def x_w(c, j, ps, eng):
+        def x_w(c, j, eng):
+            ps = w_ps[c, j]
             off = (c % 2) * 256 + j * P
             dst = gW[c // 2][:].bitcast(F32).rearrange("q (g o e) -> q g o e", g=2, e=2)[:, :, off : off + P, :]
             copy_on(eng, dst, ps[:].rearrange("q (g e o) -> q g o e", g=2, e=2))
@@ -172,17 +171,17 @@ def tile_loratacmlp4_pb_t_kernel(tc, h, z, u, b, W_out, b_out, out):
             dst = bias_sb[a][:, n * 512 : (n + 1) * 512].rearrange("q (c j p) -> q c j p", c=2, j=2)
             copy_on(eng, dst, ps[:].rearrange("q (c p j) -> q c j p", c=2, j=2))
 
-        def lo(i, t, n):
-            ps = bank([P, 512], F32, "lo_ps%d_%d_%d" % (i, t, n))
+        def lo(i, t, n, x):
+            if x == 0:
+                lo_ps[i, t, n] = bank([P, 512], F32, "lo_ps%d_%d_%d" % (i, t, n))
             q = (i % 4) * 2 + t
-            nc.tensor.matmul(out=ps[:], lhsT=zT[i // 4][:, q * P : (q + 1) * P], rhs=uT[i][:, n * 512 : (n + 1) * 512],
+            nc.tensor.matmul(out=lo_ps[i, t, n][:, x * LW : (x + 1) * LW], lhsT=zT[i // 4][:, q * P : (q + 1) * P],
+                             rhs=uT[i][:, n * 512 + x * LW : n * 512 + (x + 1) * LW],
                              start=True, stop=p1_engine(i, 2 * t + n) != "act")
-            lo_ps[i, t, n] = ps
-
-        def lo_bias(i, t, n):
-            m = (i // 8) * 2 + n
-            nc.tensor.matmul(out=lo_ps[i, t, n][:], lhsT=c128[:], rhs=bias_pm[:, m * 512 : (m + 1) * 512],
-                             start=False, stop=True)
+            if p1_engine(i, 2 * t + n) == "act":
+                m = (i // 8) * 2 + n
+                nc.tensor.matmul(out=lo_ps[i, t, n][:, x * LW : (x + 1) * LW], lhsT=c128[:],
+                                 rhs=bias_pm[:, m * 512 + x * LW : m * 512 + (x + 1) * LW], start=False, stop=True)
 
         def p1(i, t, n, eng):
             if (i not in pre):
@@ -245,66 +244,56 @@ def tile_loratacmlp4_pb_t_kernel(tc, h, z, u, b, W_out, b_out, out):
         late_ge = None
         for s in range(-DU, UNITS):
             iu, il, ih = s + DU, s + DL, s + DH
-            runs = []
-            for c in W_AT.get(s, ()):
-                for j in range(2):
-                    runs.append(("w", c, j))
-            if 0 <= ih < UNITS:
-                runs.append(("h", ih, 0))
-                runs.append(("h", ih, 1))
-            if iu % 4 == 0 and iu < UNITS:
-                runs.append(("z", iu // 4, 0))
-            if iu < UNITS:
-                runs.append(("u", iu, 0))
-                runs.append(("u", iu, 1))
             if il in (0, 8):
                 pb = [bias_mm(il // 8, n) for n in range(2)]
                 for n in range(2):
                     bias_x(il // 8, n, pb[n], "dve")
-            slots = []
+            slow, fast = [], []
+            for c in W_AT.get(s, ()):
+                for j in range(2):
+                    slow += [("w", c, j, q) for q in range(4)]
+            if 0 <= ih < UNITS:
+                slow += [("h", ih, t, q) for t in range(2) for q in range(4)]
+            if iu % 4 == 0 and iu < UNITS:
+                fast += [("z", iu // 4, 0, q) for q in range(8)]
+            if iu < UNITS:
+                fast += [("u", iu, 0, q) for q in range(8)]
+            plain = []
             if 0 <= il < UNITS:
-                for j in range(4):
-                    slots.append(("lo", j))
-                    if p1_engine(il, j) == "act":
-                        slots.append(("bias", j))
-            gaps = max(len(slots) - 1, 1)
-            per_gap = (len(runs) + gaps - 1) // gaps
-            done = 0
-            for k in range(max(len(slots), 1)):
-                if slots:
-                    kind, j = slots[k]
-                    if kind == "lo":
-                        lo(il, j // 2, j % 2)
-                    else:
-                        lo_bias(il, j // 2, j % 2)
-                    if kind == "bias" or p1_engine(il, j) != "act":
+                plain = [(j, x) for j in range(4) for x in range(512 // LW)]
+            gaps = max(len(plain) - 1, 1)
+
+            def share(lst, k):
+                return lst[len(lst) * k // gaps : len(lst) * (k + 1) // gaps]
+
+            for k in range(max(len(plain), 1)):
+                if plain:
+                    j, x = plain[k]
+                    lo(il, j // 2, j % 2, x)
+                    if x == 512 // LW - 1:
                         p1(il, j // 2, j % 2, p1_engine(il, j))
                 if k < gaps:
-                    todo = runs[done : done + per_gap]
-                    done += len(todo)
-                    held = []
-                    for kind, a, bb in todo:
-                        if kind == "w":
-                            held.append(t_w(a, bb))
-                        elif kind == "h":
-                            t_h(a, bb)
-                            held.append(None)
-                        elif kind == "z":
-                            held.append(t_z(a))
-                        else:
-                            t_u(a, bb)
-                            held.append(None)
-                    for (kind, a, bb), ps in zip(todo, held):
-                        if kind == "w":
-                            x_w(a, bb, ps, "act" if bb in XW_ACT else "dve")
-                            if bb == 1 and a % 2 == 1:
-                                q_w(a // 2)
-                        elif kind == "h":
-                            x_h(a, bb, "act")
-                        elif kind == "z":
-                            x_z(a, ps, XU_ENG)
-                        elif bb == 1:
-                            x_u(a, XU_ENG)
+                    a, b2 = share(slow, k), share(fast, k)
+                    for m in range(max(len(a), len(b2))):
+                        for kind, i, t, q in a[m : m + 1] + b2[m : m + 1]:
+                            if kind == "w":
+                                t_w(i, t, q)
+                                if q == 3:
+                                    x_w(i, t, "act" if t in XW_ACT else "dve")
+                                    if t == 1 and i % 2 == 1:
+                                        q_w(i // 2)
+                            elif kind == "h":
+                                t_h(i, t, q)
+                                if q == 3:
+                                    x_h(i, t, "act")
+                            elif kind == "z":
+                                t_z(i, q)
+                                if q == 7:
+                                    x_z(i, XU_ENG)
+                            else:
+                                t_u(i, q)
+                                if q == 7:
+                                    x_u(i, XU_ENG)
             if late_ge is not None:
                 ge(*late_ge)
                 late_ge = None

@@ -26,14 +26,12 @@ MANUAL = True
 ACT_J = [(1, 2), (1,), (1,), (1,)]
 XU_ENG = "act"
 HEAD_ACT = (1, 3)
-XW_ACT = (0,)
+XW_ACT = (0, 1)
 LW = 256
 
 
 def p1_engine(i, j):
-    if i < DL:
-        return "act" if j in HEAD_ACT else "dve"
-    return "act" if j in ACT_J[i % len(ACT_J)] else "dve"
+    return "gp" if j == 1 else "dve"
 
 
 def tile_loratacmlp4_pb_t_kernel(tc, h, z, u, b, W_out, b_out, out):
@@ -188,8 +186,10 @@ def tile_loratacmlp4_pb_t_kernel(tc, h, z, u, b, W_out, b_out, out):
                 pre[i] = prep.tile([P, 2048], F32, name="pre_%d" % i, tag="pre")
             dst = pre[i][:, t * 1024 + n * 512 : t * 1024 + (n + 1) * 512]
             bia = bias_sb[i // 8][:, n * 512 : (n + 1) * 512]
-            if eng == "act":
+            if eng in ("act", "gp"):
                 nc.scalar.activation(out=dst, in_=lo_ps[i, t, n][:], func=ACTF.Copy, scale=1.0 / 128.0)
+                if eng == "gp":
+                    nc.gpsimd.tensor_tensor(out=dst, in0=dst, in1=bia, op=ALU.add)
             else:
                 nc.vector.scalar_tensor_tensor(out=dst, in0=lo_ps[i, t, n][:], scalar=1.0 / 128.0, in1=bia,
                                                op0=ALU.mult, op1=ALU.add)
@@ -247,7 +247,7 @@ def tile_loratacmlp4_pb_t_kernel(tc, h, z, u, b, W_out, b_out, out):
             if il in (0, 8):
                 pb = [bias_mm(il // 8, n) for n in range(2)]
                 for n in range(2):
-                    bias_x(il // 8, n, pb[n], "dve")
+                    bias_x(il // 8, n, pb[n], "act")
             slow, fast = [], []
             for c in W_AT.get(s, ()):
                 for j in range(2):

@@ -20,13 +20,23 @@ DL = 4
 DH = 2
 PRE_BUFS = 6
 W_STEP = -2.5
-W_AT = {-3: (0, 1), -2: (2, 3)}
+W_AT = {-4: (0,), -3: (1,), -2: (2,), -1: (3,)}
+Z_AT = {-3: 1, 2: 2, 6: 3}
+Z0B = -4
+ZO = 0.2
+WL0 = -4.5
+WL1 = 0.7
+BIAS_AT = -5
 LOAD_AHEAD = 3
 MANUAL = True
 ACT_J = [(1, 2), (1,), (1,), (1,)]
 XU_ENG = "act"
 HEAD_ACT = (1, 3)
-XW_ACT = (0, 1)
+XW_ACT = (0,)
+NB = 1
+BX = "act"
+GE1 = 0
+GE0 = 2
 LW = 256
 
 
@@ -58,26 +68,26 @@ def tile_loratacmlp4_pb_t_kernel(tc, h, z, u, b, W_out, b_out, out):
         def bank(shape, dtype, name):
             return psum.tile(shape, dtype, name=name, tag="ps")
 
+        zeros = const.tile([P, 512], BF16, name="zeros")
+        nc.vector.memset(zeros[:], 0.0)
+        for k in range(5):
+            warm_ps = bank([P, 512], F32, "b_warm%d" % k)
+            nc.tensor.matmul(out=warm_ps[:], lhsT=zeros[:, :P], rhs=zeros[:], start=True, stop=True)
+
+        bias_in = const.tile([P, 2, 1024], BF16, name="bias_in")
+        nc.vector.memset(bias_in[:].bitcast(F32), 0.0)
+        for a in range(2):
+            nc.scalar.dma_start(out=bias_in[0:1, a, :], in_=bo_v)
+        nc.scalar.dma_start(out=bias_in[1:2, :, :], in_=b_v)
+        ones = const.tile([P, P], BF16, name="ones")
+        nc.vector.memset(ones[:], 1.0)
+        warm = const.tile([P, 1], F32, name="warm")
+        nc.vector.memset(warm[:], 0.0)
+        nc.scalar.activation(out=warm[:], in_=warm[:], func=ACTF.Gelu)
         ident_f = const.tile([P, P], F32, name="ident_f")
         ident_b = const.tile([P, P], BF16, name="ident_b")
         make_identity(nc, ident_b[:])
         make_identity(nc, ident_f[:])
-        ones = const.tile([P, P], BF16, name="ones")
-        nc.vector.memset(ones[:], 1.0)
-        bias_in = const.tile([P, 2, 1024], BF16, name="bias_in")
-        nc.vector.memset(bias_in[:], 0.0)
-        c128 = const.tile([P, P], BF16, name="c128")
-        nc.vector.memset(c128[:], 128.0)
-        bias_pm = const.tile([P, 2048], BF16, name="bias_pm")
-        warm = const.tile([P, 1], F32, name="warm")
-        nc.vector.memset(warm[:], 0.0)
-        nc.scalar.activation(out=warm[:], in_=warm[:], func=ACTF.Gelu)
-        nc.scalar.dma_start(out=bias_in[1:2, :, :], in_=b_v)
-        for a in range(2):
-            nc.scalar.dma_start(out=bias_in[0:1, a, :], in_=bo_v)
-
-        nc.vector.tensor_copy(out=bias_pm[:].rearrange("q (m j p) -> q m j p", m=8, j=2),
-                              in_=bias_in[:].rearrange("q a (c p j) -> q (a c) j p", c=4, j=2))
 
         z_sb = [const.tile([P, 4, 256], BF16, name="z_sb%d" % k) for k in range(4)]
         zT = [const.tile([P, 1024], BF16, name="zT%d" % k) for k in range(4)]
@@ -89,8 +99,8 @@ def tile_loratacmlp4_pb_t_kernel(tc, h, z, u, b, W_out, b_out, out):
 
         h_sb, u_sb, hq, ch, sh, uT, pre, lo_ps, mx_ps, h_ps, u_ps, z_ps, w_ps = ({} for _ in range(13))
 
-        def load_z(k):
-            nc.sync.dma_start(out=z_sb[k][:], in_=z_v[:, 4 * k : 4 * k + 4, :])
+        def load_z(k, lo_i=0, hi_i=4):
+            nc.sync.dma_start(out=z_sb[k][:, lo_i:hi_i, :], in_=z_v[:, 4 * k + lo_i : 4 * k + hi_i, :])
 
         def load_w(c):
             nc.sync.dma_start(out=w_sb[c][:], in_=w_v[c])
@@ -110,12 +120,12 @@ def tile_loratacmlp4_pb_t_kernel(tc, h, z, u, b, W_out, b_out, out):
                 nc.vector.tensor_copy(out=out_, in_=in_)
 
         def t_z(k, q):
-            if q == 0:
-                z_ps[k] = bank([P, 1024], BF16, "z_ps%d" % k)
+            if q == 0 or (k == 0 and q == 2):
+                z_ps[k] = bank([P, 1024], BF16, "z_ps%d_%d" % (k, q))
             nc.tensor.transpose(z_ps[k][:, q * P : (q + 1) * P], z_sb[k][:, q // 2, (q % 2) * P : (q % 2 + 1) * P], ident_b[:])
 
-        def x_z(k, eng):
-            copy_on(eng, zT[k][:], z_ps[k][:])
+        def x_z(k, lo_q, hi_q, eng):
+            copy_on(eng, zT[k][:, lo_q * P : hi_q * P], z_ps[k][:, lo_q * P : hi_q * P])
 
         def t_u(i, q):
             if q == 0:
@@ -175,11 +185,7 @@ def tile_loratacmlp4_pb_t_kernel(tc, h, z, u, b, W_out, b_out, out):
             q = (i % 4) * 2 + t
             nc.tensor.matmul(out=lo_ps[i, t, n][:, x * LW : (x + 1) * LW], lhsT=zT[i // 4][:, q * P : (q + 1) * P],
                              rhs=uT[i][:, n * 512 + x * LW : n * 512 + (x + 1) * LW],
-                             start=True, stop=p1_engine(i, 2 * t + n) != "act")
-            if p1_engine(i, 2 * t + n) == "act":
-                m = (i // 8) * 2 + n
-                nc.tensor.matmul(out=lo_ps[i, t, n][:, x * LW : (x + 1) * LW], lhsT=c128[:],
-                                 rhs=bias_pm[:, m * 512 + x * LW : m * 512 + (x + 1) * LW], start=False, stop=True)
+                             start=True, stop=True)
 
         def p1(i, t, n, eng):
             if (i not in pre):
@@ -223,56 +229,69 @@ def tile_loratacmlp4_pb_t_kernel(tc, h, z, u, b, W_out, b_out, out):
                                  func=ACTF.Gelu)
             nc.sync.dma_start(out=o_v[i][:, t, n * 512 : (n + 1) * 512], in_=st[:])
 
-        loads = []
+        loads = [(-9, 0, load_z, 0, 0, 1), (-8, 0, load_u, 0), (-7.5, 0, load_z, 0, 1, 4)]
         for i in range(UNITS):
-            loads.append((i - DU, 1, load_u, i))
+            if i:
+                loads.append((i - DU, 1, load_u, i))
             loads.append((i - DH, 2, load_h, i))
-        for kk in range(4):
-            loads.append((4 * kk - DU, 0, load_z, kk))
+        for kk in range(1, 4):
+            loads.append(([k for k in Z_AT if Z_AT[k] == kk][0] - ZO, 0, load_z, kk))
         for c in range(4):
-            loads.append((W_STEP - 0.5, c, load_w, c))
+            loads.append((WL0 + WL1 * c, 3, load_w, c))
         loads = sorted(loads, key=lambda e: (e[0], e[1]))
         issued = [0]
 
         def issue_loads(upto):
             while issued[0] < len(loads) and loads[issued[0]][0] <= upto:
                 e = loads[issued[0]]
-                e[2](e[3])
+                e[2](*e[3:])
                 issued[0] += 1
 
         issue_loads(-DU + LOAD_AHEAD)
-        late_ge = None
+        head_slow = [("w", c, j, q) for c in range(4) for j in range(2) for q in range(4)]
+        head_slow += [("h", i, t, q) for i in range(DH) for t in range(2) for q in range(4)]
+        HS = len(head_slow) // DL
         for s in range(-DU, UNITS):
             iu, il, ih = s + DU, s + DL, s + DH
-            if il in (0, 8):
-                pb = [bias_mm(il // 8, n) for n in range(2)]
+            if s == BIAS_AT or il == 8:
+                a = int(il == 8)
+                pb = [bias_mm(a, n) for n in range(2)]
                 for n in range(2):
-                    bias_x(il // 8, n, pb[n], "act")
-            slow, fast = [], []
-            for c in W_AT.get(s, ()):
-                for j in range(2):
-                    slow += [("w", c, j, q) for q in range(4)]
-            if 0 <= ih < UNITS:
-                slow += [("h", ih, t, q) for t in range(2) for q in range(4)]
-            if iu % 4 == 0 and iu < UNITS:
-                fast += [("z", iu // 4, 0, q) for q in range(8)]
+                    bias_x(a, n, pb[n], BX if a else "dve")
+            fast = []
+            if s < 0:
+                slow = head_slow[HS * (s + DL) : HS * (s + DL + 1)] if s >= -DL else []
+            elif ih < UNITS:
+                slow = [("h", ih, t, q) for t in range(2) for q in range(4)]
+            else:
+                slow = []
+            if s == -DU:
+                fast += [("z", 0, 0, q) for q in range(2)]
+            if s == Z0B:
+                fast += [("z", 0, 0, q) for q in range(2, 8)]
+            if s in Z_AT:
+                fast += [("z", Z_AT[s], 0, q) for q in range(8)]
             if iu < UNITS:
                 fast += [("u", iu, 0, q) for q in range(8)]
+            nb = NB if s >= 0 else 1
+            npc = 512 // LW
             plain = []
             if 0 <= il < UNITS:
-                plain = [(j, x) for j in range(4) for x in range(512 // LW)]
-            gaps = max(len(plain) - 1, 1)
+                plain = [(j, x) for j in range(4) for x in range(npc)]
+            per = max(len(plain) // nb, 1)
+            gaps = [k for k in range(max(len(plain), 1)) if (k + 1) % per or not plain]
 
             def share(lst, k):
-                return lst[len(lst) * k // gaps : len(lst) * (k + 1) // gaps]
+                m = gaps.index(k)
+                return lst[len(lst) * m // len(gaps) : len(lst) * (m + 1) // len(gaps)]
 
-            for k in range(max(len(plain), 1)):
+            for k in range(max(len(plain), nb)):
                 if plain:
                     j, x = plain[k]
                     lo(il, j // 2, j % 2, x)
-                    if x == 512 // LW - 1:
+                    if x == npc - 1:
                         p1(il, j // 2, j % 2, p1_engine(il, j))
-                if k < gaps:
+                if k in gaps:
                     a, b2 = share(slow, k), share(fast, k)
                     for m in range(max(len(a), len(b2))):
                         for kind, i, t, q in a[m : m + 1] + b2[m : m + 1]:
@@ -286,28 +305,30 @@ def tile_loratacmlp4_pb_t_kernel(tc, h, z, u, b, W_out, b_out, out):
                                 t_h(i, t, q)
                                 if q == 3:
                                     x_h(i, t, "act")
+                                    if s < 0 and t == 1:
+                                        q_h(i)
                             elif kind == "z":
                                 t_z(i, q)
-                                if q == 7:
-                                    x_z(i, XU_ENG)
+                                if i == 0 and q == 1:
+                                    x_z(0, 0, 2, XU_ENG)
+                                elif q == 7:
+                                    x_z(i, 2 if i == 0 else 0, 8, "dve" if i == 0 else XU_ENG)
                             else:
                                 t_u(i, q)
                                 if q == 7:
                                     x_u(i, XU_ENG)
-            if late_ge is not None:
-                ge(*late_ge)
-                late_ge = None
+                if s >= 0 and (k + 1) % per == 0:
+                    hb = k // per
+                    for j in range(4 * hb // nb, 4 * (hb + 1) // nb):
+                        t, n = j // 2, j % 2
+                        mx(s, t, n)
+                        p2(s, t, n)
+                        if j == GE1 and s > 0 and s < UNITS:
+                            ge(s - 1, 1)
+                        if s == UNITS - 1:
+                            ge_half(s, t, n)
+                        elif j == GE0:
+                            ge(s, 0)
             issue_loads(s + 1 + LOAD_AHEAD)
-            for j in range(4):
-                t, n = j // 2, j % 2
-                if s >= 0:
-                    mx(s, t, n)
-                    p2(s, t, n)
-                    if s == UNITS - 1:
-                        ge_half(s, t, n)
-                    elif j == 1:
-                        ge(s, 0)
-            if 0 <= ih < UNITS:
+            if s >= 0 and ih < UNITS:
                 q_h(ih)
-            if 0 <= s < UNITS - 1:
-                late_ge = (s, 1)

@@ -18,7 +18,7 @@ UNITS = 16
 DU = 6
 DL = 4
 DH = 2
-PRE_BUFS = 6
+PRE_BUFS = 7
 W_STEP = -2.5
 W_AT = {-4: (0,), -3: (1,), -2: (2,), -1: (3,)}
 Z_AT = {-3: 1, 2: 2, 6: 3}
@@ -27,6 +27,7 @@ ZO = 0.2
 WL0 = -4.5
 WL1 = 0.7
 BIAS_AT = -5
+BIAS1_AT = 0
 LOAD_AHEAD = 3
 MANUAL = True
 ACT_J = [(1, 2), (1,), (1,), (1,)]
@@ -34,14 +35,16 @@ XU_ENG = "act"
 HEAD_ACT = (1, 3)
 XW_ACT = (0,)
 NB = 1
+QW = 1
+QH = 1
 BX = "act"
 GE1 = 0
 GE0 = 2
-LW = 256
+LW = 512
 
 
 def p1_engine(i, j):
-    return "gp" if j == 1 else "dve"
+    return "gp" if j == 1 or (j == 3 and i in (12, 14)) else "dve"
 
 
 def tile_loratacmlp4_pb_t_kernel(tc, h, z, u, b, W_out, b_out, out):
@@ -58,7 +61,7 @@ def tile_loratacmlp4_pb_t_kernel(tc, h, z, u, b, W_out, b_out, out):
         const = ctx.enter_context(tc.tile_pool(name="const", bufs=1))
         hpool = ctx.enter_context(tc.tile_pool(name="hpool", bufs=8))
         upool = ctx.enter_context(tc.tile_pool(name="upool", bufs=8))
-        work = ctx.enter_context(tc.tile_pool(name="work", bufs=3))
+        work = ctx.enter_context(tc.tile_pool(name="work", bufs=4))
         prep = ctx.enter_context(tc.tile_pool(name="prep", bufs=PRE_BUFS))
         stg = ctx.enter_context(tc.tile_pool(name="stg", bufs=6))
         psum = ctx.enter_context(tc.psum_pool(name="psum", bufs=8))
@@ -251,10 +254,11 @@ def tile_loratacmlp4_pb_t_kernel(tc, h, z, u, b, W_out, b_out, out):
         head_slow = [("w", c, j, q) for c in range(4) for j in range(2) for q in range(4)]
         head_slow += [("h", i, t, q) for i in range(DH) for t in range(2) for q in range(4)]
         HS = len(head_slow) // DL
+        later = []
         for s in range(-DU, UNITS):
             iu, il, ih = s + DU, s + DL, s + DH
-            if s == BIAS_AT or il == 8:
-                a = int(il == 8)
+            if s == BIAS_AT or s == BIAS1_AT:
+                a = int(s == BIAS1_AT)
                 pb = [bias_mm(a, n) for n in range(2)]
                 for n in range(2):
                     bias_x(a, n, pb[n], BX if a else "dve")
@@ -291,6 +295,11 @@ def tile_loratacmlp4_pb_t_kernel(tc, h, z, u, b, W_out, b_out, out):
                     lo(il, j // 2, j % 2, x)
                     if x == npc - 1:
                         p1(il, j // 2, j % 2, p1_engine(il, j))
+                        for e in list(later):
+                            e[0] -= 1
+                            if e[0] <= 0:
+                                later.remove(e)
+                                e[1](e[2])
                 if k in gaps:
                     a, b2 = share(slow, k), share(fast, k)
                     for m in range(max(len(a), len(b2))):
@@ -300,13 +309,13 @@ def tile_loratacmlp4_pb_t_kernel(tc, h, z, u, b, W_out, b_out, out):
                                 if q == 3:
                                     x_w(i, t, "act" if t in XW_ACT else "dve")
                                     if t == 1 and i % 2 == 1:
-                                        q_w(i // 2)
+                                        later.append([QW, q_w, i // 2])
                             elif kind == "h":
                                 t_h(i, t, q)
                                 if q == 3:
                                     x_h(i, t, "act")
                                     if s < 0 and t == 1:
-                                        q_h(i)
+                                        later.append([QH, q_h, i])
                             elif kind == "z":
                                 t_z(i, q)
                                 if i == 0 and q == 1:
@@ -318,6 +327,9 @@ def tile_loratacmlp4_pb_t_kernel(tc, h, z, u, b, W_out, b_out, out):
                                 if q == 7:
                                     x_u(i, XU_ENG)
                 if s >= 0 and (k + 1) % per == 0:
+                    for e in later:
+                        e[1](e[2])
+                    later = []
                     hb = k // per
                     for j in range(4 * hb // nb, 4 * (hb + 1) // nb):
                         t, n = j // 2, j % 2

from contextlib import ExitStack

import concourse.mybir as mybir
from concourse.masks import make_identity

F32 = mybir.dt.float32
BF16 = mybir.dt.bfloat16
U32 = mybir.dt.uint32
U8 = mybir.dt.uint8
FP8X4 = mybir.dt.float8_e4m3fn_x4
ACTF = mybir.ActivationFunctionType
ALU = mybir.AluOpType

FLOPS = 2 * 4096 * 1024 * 1024 + 2 * 4096 * 1024 * 128

P = 128
UNITS = 16
DU = 6
DL = 4
DH = 2
PRE_BUFS = 7
W_STEP = -2.5
W_AT = {-4: (0,), -3: (1,), -2: (2,), -1: (3,)}
Z_AT = {-3: 1, 2: 2, 6: 3}
Z0B = -4
ZO = 0.2
WL0 = -4.5
WL1 = 0.7
BIAS_AT = -5
BIAS1_AT = 0
LOAD_AHEAD = 3
MANUAL = True
ACT_J = [(1, 2), (1,), (1,), (1,)]
XU_ENG = "act"
HEAD_ACT = (1, 3)
XW_ACT = (0,)
NB = 1
QW = 1
QH = 1
BX = "act"
GE1 = 0
GE0 = 2
LW = 512


def p1_engine(i, j):
    return "gp" if j == 1 or (j == 3 and i in (12, 14)) else "dve"


def tile_loratacmlp4_pb_t_kernel(tc, h, z, u, b, W_out, b_out, out):
    nc = tc.nc
    h_v = h.rearrange("a k (p t) c -> (a k) p (t c)", t=2)
    z_v = z.rearrange("a k (p t) r -> p (a k) (t r)", t=2)
    u_v = u.rearrange("a k (c p j) r -> (a k) p c (j r)", c=4, j=2)
    w_v = W_out.rearrange("(c p j) k -> c p (j k)", c=4, j=2)
    o_v = out.rearrange("a k (p t) o -> (a k) p t o", t=2)
    b_v = b.rearrange("a x y o -> (x y) a o")
    bo_v = b_out.rearrange("(x o) -> x o", x=1)

    with ExitStack() as ctx:
        const = ctx.enter_context(tc.tile_pool(name="const", bufs=1))
        hpool = ctx.enter_context(tc.tile_pool(name="hpool", bufs=8))
        upool = ctx.enter_context(tc.tile_pool(name="upool", bufs=8))
        work = ctx.enter_context(tc.tile_pool(name="work", bufs=4))
        prep = ctx.enter_context(tc.tile_pool(name="prep", bufs=PRE_BUFS))
        stg = ctx.enter_context(tc.tile_pool(name="stg", bufs=6))
        psum = ctx.enter_context(tc.psum_pool(name="psum", bufs=8))
        if MANUAL:
            ctx.enter_context(tc.manual_schedule())

        def bank(shape, dtype, name):
            return psum.tile(shape, dtype, name=name, tag="ps")

        zeros = const.tile([P, 512], BF16, name="zeros")
        nc.vector.memset(zeros[:], 0.0)
        for k in range(5):
            warm_ps = bank([P, 512], F32, "b_warm%d" % k)
            nc.tensor.matmul(out=warm_ps[:], lhsT=zeros[:, :P], rhs=zeros[:], start=True, stop=True)

        bias_in = const.tile([P, 2, 1024], BF16, name="bias_in")
        nc.vector.memset(bias_in[:].bitcast(F32), 0.0)
        for a in range(2):
            nc.scalar.dma_start(out=bias_in[0:1, a, :], in_=bo_v)
        nc.scalar.dma_start(out=bias_in[1:2, :, :], in_=b_v)
        ones = const.tile([P, P], BF16, name="ones")
        nc.vector.memset(ones[:], 1.0)
        warm = const.tile([P, 1], F32, name="warm")
        nc.vector.memset(warm[:], 0.0)
        nc.scalar.activation(out=warm[:], in_=warm[:], func=ACTF.Gelu)
        ident_f = const.tile([P, P], F32, name="ident_f")
        ident_b = const.tile([P, P], BF16, name="ident_b")
        make_identity(nc, ident_b[:])
        make_identity(nc, ident_f[:])

        z_sb = [const.tile([P, 4, 256], BF16, name="z_sb%d" % k) for k in range(4)]
        zT = [const.tile([P, 1024], BF16, name="zT%d" % k) for k in range(4)]
        w_sb = [const.tile([P, 2048], BF16, name="w_sb%d" % c) for c in range(4)]
        gW = [const.tile([P, 4096], BF16, name="gW%d" % n, align_bytes=64) for n in range(2)]
        cW = [const.tile([P, 1024], U32, name="cW%d" % n, align_bytes=64) for n in range(2)]
        sW = [const.tile([P, 1024], U8, name="sW%d" % n, align_bytes=64) for n in range(2)]
        bias_sb = [const.tile([P, 1024], F32, name="bias_sb%d" % a) for a in range(2)]

        h_sb, u_sb, hq, ch, sh, uT, pre, lo_ps, mx_ps, h_ps, u_ps, z_ps, w_ps = ({} for _ in range(13))

        def load_z(k, lo_i=0, hi_i=4):
            nc.sync.dma_start(out=z_sb[k][:, lo_i:hi_i, :], in_=z_v[:, 4 * k + lo_i : 4 * k + hi_i, :])

        def load_w(c):
            nc.sync.dma_start(out=w_sb[c][:], in_=w_v[c])

        def load_u(i):
            u_sb[i] = upool.tile([P, 4, 256], BF16, name="u_sb_%d" % i, tag="u")
            nc.sync.dma_start(out=u_sb[i][:], in_=u_v[i])

        def load_h(i):
            h_sb[i] = hpool.tile([P, 2048], BF16, name="h_sb_%d" % i, tag="h")
            nc.sync.dma_start(out=h_sb[i][:], in_=h_v[i])

        def copy_on(eng, out_, in_):
            if eng == "act":
                nc.scalar.copy(out=out_, in_=in_)
            else:
                nc.vector.tensor_copy(out=out_, in_=in_)

        def t_z(k, q):
            if q == 0 or (k == 0 and q == 2):
                z_ps[k] = bank([P, 1024], BF16, "z_ps%d_%d" % (k, q))
            nc.tensor.transpose(z_ps[k][:, q * P : (q + 1) * P], z_sb[k][:, q // 2, (q % 2) * P : (q % 2 + 1) * P], ident_b[:])

        def x_z(k, lo_q, hi_q, eng):
            copy_on(eng, zT[k][:, lo_q * P : hi_q * P], z_ps[k][:, lo_q * P : hi_q * P])

        def t_u(i, q):
            if q == 0:
                u_ps[i] = bank([P, 1024], BF16, "u_ps%d" % i)
            nc.tensor.transpose(u_ps[i][:, q * P : (q + 1) * P], u_sb[i][:, q // 2, (q % 2) * P : (q % 2 + 1) * P], ident_b[:])

        def x_u(i, eng):
            uT[i] = work.tile([P, 1024], BF16, name="uT_%d" % i, tag="uT", bufs=4)
            copy_on(eng, uT[i][:], u_ps[i][:])

        def word_T(ps, src_f32, base, q):
            at = base + (q // 2) * 256 + q % 2
            nc.tensor.transpose(ps[:, q * P : (q + 1) * P], src_f32[:, at : at + 255 : 2], ident_f[:])

        def t_h(i, t, q):
            if q == 0:
                h_ps[i, t] = bank([P, 512], F32, "h_ps%d_%d" % (i, t))
            word_T(h_ps[i, t], h_sb[i][:].bitcast(F32), t * 512, q)

        def x_h(i, t, eng):
            if t == 0:
                hq[i] = work.tile([P, 2048], BF16, name="hq_%d" % i, tag="hq", align_bytes=64)
            dst = hq[i][:].bitcast(F32)[:, t * 512 : (t + 1) * 512].rearrange("q (g f e) -> q g f e", g=2, e=2)
            copy_on(eng, dst, h_ps[i, t][:].rearrange("q (g e f) -> q g f e", g=2, e=2))

        def q_h(i):
            ch[i] = work.tile([P, 512], U32, name="ch_%d" % i, tag="ch", align_bytes=64)
            sh[i] = work.tile([P, 512], U8, name="sh_%d" % i, tag="sh", align_bytes=64)
            nc.vector.quantize_mx(out=ch[i][:].bitcast(FP8X4), scales=sh[i][:], in_=hq[i][:])

        def t_w(c, j, q):
            if q == 0:
                w_ps[c, j] = bank([P, 512], F32, "w_ps%d_%d" % (c, j))
            word_T(w_ps[c, j], w_sb[c][:].bitcast(F32), j * 512, q)

        def x_w(c, j, eng):
            ps = w_ps[c, j]
            off = (c % 2) * 256 + j * P
            dst = gW[c // 2][:].bitcast(F32).rearrange("q (g o e) -> q g o e", g=2, e=2)[:, :, off : off + P, :]
            copy_on(eng, dst, ps[:].rearrange("q (g e o) -> q g o e", g=2, e=2))

        def q_w(n):
            nc.vector.quantize_mx(out=cW[n][:].bitcast(FP8X4), scales=sW[n][:], in_=gW[n][:])

        def bias_mm(a, n):
            ps = bank([P, 512], F32, "b_ps%d_%d" % (a, n))
            nc.tensor.matmul(out=ps[:], lhsT=ones[:], rhs=bias_in[:, a, n * 512 : (n + 1) * 512], start=True, stop=True)
            return ps

        def bias_x(a, n, ps, eng):
            dst = bias_sb[a][:, n * 512 : (n + 1) * 512].rearrange("q (c j p) -> q c j p", c=2, j=2)
            copy_on(eng, dst, ps[:].rearrange("q (c p j) -> q c j p", c=2, j=2))

        def lo(i, t, n, x):
            if x == 0:
                lo_ps[i, t, n] = bank([P, 512], F32, "lo_ps%d_%d_%d" % (i, t, n))
            q = (i % 4) * 2 + t
            nc.tensor.matmul(out=lo_ps[i, t, n][:, x * LW : (x + 1) * LW], lhsT=zT[i // 4][:, q * P : (q + 1) * P],
                             rhs=uT[i][:, n * 512 + x * LW : n * 512 + (x + 1) * LW],
                             start=True, stop=True)

        def p1(i, t, n, eng):
            if (i not in pre):
                pre[i] = prep.tile([P, 2048], F32, name="pre_%d" % i, tag="pre")
            dst = pre[i][:, t * 1024 + n * 512 : t * 1024 + (n + 1) * 512]
            bia = bias_sb[i // 8][:, n * 512 : (n + 1) * 512]
            if eng in ("act", "gp"):
                nc.scalar.activation(out=dst, in_=lo_ps[i, t, n][:], func=ACTF.Copy, scale=1.0 / 128.0)
                if eng == "gp":
                    nc.gpsimd.tensor_tensor(out=dst, in0=dst, in1=bia, op=ALU.add)
            else:
                nc.vector.scalar_tensor_tensor(out=dst, in0=lo_ps[i, t, n][:], scalar=1.0 / 128.0, in1=bia,
                                               op0=ALU.mult, op1=ALU.add)

        def mx(i, t, n):
            ps = bank([P, 512], F32, "mx_ps%d_%d_%d" % (i, t, n))
            for g in range(2):
                q = 2 * t + g
                nc.tensor.matmul_mx(out=ps[:], lhsT=ch[i][:, q * P : (q + 1) * P].bitcast(FP8X4),
                                    lhsT_scale=sh[i][:, q * P : (q + 1) * P],
                                    rhs=cW[n][:, g * 512 : (g + 1) * 512].bitcast(FP8X4),
                                    rhs_scale=sW[n][:, g * 512 : (g + 1) * 512], start=(g == 0), stop=(g == 1))
            mx_ps[i, t, n] = ps

        def p2(i, t, n):
            dst = pre[i][:, t * 1024 + n * 512 : t * 1024 + (n + 1) * 512]
            nc.vector.tensor_tensor(out=dst, in0=mx_ps[i, t, n][:], in1=dst, op=ALU.add)

        def ge(i, t):
            st = stg.tile([P, 1024], F32, name="st_%d_%d" % (i, t), tag="st")
            nc.scalar.activation(out=st[:].rearrange("q (c p j) -> q c p j", c=4, j=2),
                                 in_=pre[i][:, t * 1024 : (t + 1) * 1024].rearrange("q (c j p) -> q c p j", c=4, j=2),
                                 func=ACTF.Gelu)
            nc.sync.dma_start(out=o_v[i][:, t, :], in_=st[:])

        def ge_half(i, t, n):
            st = stg.tile([P, 512], F32, name="sth_%d_%d_%d" % (i, t, n), tag="st")
            lo_c = t * 1024 + n * 512
            nc.scalar.activation(out=st[:].rearrange("q (c p j) -> q c p j", c=2, j=2),
                                 in_=pre[i][:, lo_c : lo_c + 512].rearrange("q (c j p) -> q c p j", c=2, j=2),
                                 func=ACTF.Gelu)
            nc.sync.dma_start(out=o_v[i][:, t, n * 512 : (n + 1) * 512], in_=st[:])

        loads = [(-9, 0, load_z, 0, 0, 1), (-8, 0, load_u, 0), (-7.5, 0, load_z, 0, 1, 4)]
        for i in range(UNITS):
            if i:
                loads.append((i - DU, 1, load_u, i))
            loads.append((i - DH, 2, load_h, i))
        for kk in range(1, 4):
            loads.append(([k for k in Z_AT if Z_AT[k] == kk][0] - ZO, 0, load_z, kk))
        for c in range(4):
            loads.append((WL0 + WL1 * c, 3, load_w, c))
        loads = sorted(loads, key=lambda e: (e[0], e[1]))
        issued = [0]

        def issue_loads(upto):
            while issued[0] < len(loads) and loads[issued[0]][0] <= upto:
                e = loads[issued[0]]
                e[2](*e[3:])
                issued[0] += 1

        issue_loads(-DU + LOAD_AHEAD)
        head_slow = [("w", c, j, q) for c in range(4) for j in range(2) for q in range(4)]
        head_slow += [("h", i, t, q) for i in range(DH) for t in range(2) for q in range(4)]
        HS = len(head_slow) // DL
        later = []
        for s in range(-DU, UNITS):
            iu, il, ih = s + DU, s + DL, s + DH
            if s == BIAS_AT or s == BIAS1_AT:
                a = int(s == BIAS1_AT)
                pb = [bias_mm(a, n) for n in range(2)]
                for n in range(2):
                    bias_x(a, n, pb[n], BX if a else "dve")
            fast = []
            if s < 0:
                slow = head_slow[HS * (s + DL) : HS * (s + DL + 1)] if s >= -DL else []
            elif ih < UNITS:
                slow = [("h", ih, t, q) for t in range(2) for q in range(4)]
            else:
                slow = []
            if s == -DU:
                fast += [("z", 0, 0, q) for q in range(2)]
            if s == Z0B:
                fast += [("z", 0, 0, q) for q in range(2, 8)]
            if s in Z_AT:
                fast += [("z", Z_AT[s], 0, q) for q in range(8)]
            if iu < UNITS:
                fast += [("u", iu, 0, q) for q in range(8)]
            nb = NB if s >= 0 else 1
            npc = 512 // LW
            plain = []
            if 0 <= il < UNITS:
                plain = [(j, x) for j in range(4) for x in range(npc)]
            per = max(len(plain) // nb, 1)
            gaps = [k for k in range(max(len(plain), 1)) if (k + 1) % per or not plain]

            def share(lst, k):
                m = gaps.index(k)
                return lst[len(lst) * m // len(gaps) : len(lst) * (m + 1) // len(gaps)]

            for k in range(max(len(plain), nb)):
                if plain:
                    j, x = plain[k]
                    lo(il, j // 2, j % 2, x)
                    if x == npc - 1:
                        p1(il, j // 2, j % 2, p1_engine(il, j))
                        for e in list(later):
                            e[0] -= 1
                            if e[0] <= 0:
                                later.remove(e)
                                e[1](e[2])
                if k in gaps:
                    a, b2 = share(slow, k), share(fast, k)
                    for m in range(max(len(a), len(b2))):
                        for kind, i, t, q in a[m : m + 1] + b2[m : m + 1]:
                            if kind == "w":
                                t_w(i, t, q)
                                if q == 3:
                                    x_w(i, t, "act" if t in XW_ACT else "dve")
                                    if t == 1 and i % 2 == 1:
                                        later.append([QW, q_w, i // 2])
                            elif kind == "h":
                                t_h(i, t, q)
                                if q == 3:
                                    x_h(i, t, "act")
                                    if s < 0 and t == 1:
                                        later.append([QH, q_h, i])
                            elif kind == "z":
                                t_z(i, q)
                                if i == 0 and q == 1:
                                    x_z(0, 0, 2, XU_ENG)
                                elif q == 7:
                                    x_z(i, 2 if i == 0 else 0, 8, "dve" if i == 0 else XU_ENG)
                            else:
                                t_u(i, q)
                                if q == 7:
                                    x_u(i, XU_ENG)
                if s >= 0 and (k + 1) % per == 0:
                    for e in later:
                        e[1](e[2])
                    later = []
                    hb = k // per
                    for j in range(4 * hb // nb, 4 * (hb + 1) // nb):
                        t, n = j // 2, j % 2
                        mx(s, t, n)
                        p2(s, t, n)
                        if j == GE1 and s > 0 and s < UNITS:
                            ge(s - 1, 1)
                        if s == UNITS - 1:
                            ge_half(s, t, n)
                        elif j == GE0:
                            ge(s, 0)
            issue_loads(s + 1 + LOAD_AHEAD)
            if s >= 0 and ih < UNITS:
                q_h(ih)
